import numpy as np
import ml_dtypes


def mxq(x, axis, fmt="e4m3"):
    dtype, down = {"e4m3": (ml_dtypes.float8_e4m3fn, 7), "e5m2": (ml_dtypes.float8_e5m2, 14)}[fmt]
    v = np.moveaxis(np.asarray(x, np.float32).astype(ml_dtypes.bfloat16).astype(np.float64), axis, -1)
    blocks = v.reshape(v.shape[:-1] + (-1, 32))
    amax = np.abs(blocks).max(-1, keepdims=True)
    byte = np.maximum(np.where(amax > 0, np.frexp(amax)[1] - 1 + 127, 0) - down, 1)
    scale = np.exp2(byte - 127.0)
    codes = (blocks / scale).astype(np.float32).astype(dtype).astype(np.float64)
    return np.moveaxis((codes * scale).reshape(v.shape), -1, axis)


WIDE = False


def mx_kscale(k):
    if not WIDE:
        return np.ones(k)
    levels = np.array([10, -10, 5, -5, 0])
    a = np.random.permutation(np.resize(levels, k // 512 * 4)).reshape(k // 512, 4)
    idx = np.arange(k)
    return np.exp2(a[idx // 512, idx % 128 // 32])


BF16 = ml_dtypes.bfloat16


def bf(x):
    return np.asarray(x, np.float32).astype(BF16)


def f64(x):
    return np.asarray(x).astype(np.float64)


ND, NS, D0, D1, D2, D3, DH, C = 8192, 1024, 512, 512, 256, 512, 256, 10
SIG = 4.0


def draw_adj():
    w = np.exp(SIG * np.random.standard_normal((ND, NS)))
    return w / w.sum(1, keepdims=True)


def setup_inputs():
    s = mx_kscale(D0)
    return {"x": bf(np.random.standard_normal((NS, D0)) * s),
            "adj": bf(draw_adj()),
            "W0": bf(np.random.standard_normal((D0, D1)) * 2.0 / np.sqrt(D0) / s[:, None]),
            "b0": bf(np.random.standard_normal(D1) * 0.5)}


def reference(x, adj, W0, b0):
    h = (mxq(f64(x), 1, "e4m3") @ mxq(f64(W0), 0, "e4m3")) + f64(b0)
    return np.maximum(mxq(f64(adj), 1, "e4m3") @ mxq(h, 0, "e4m3"), 0.0)

@@ -1,0 +1,200 @@
+from contextlib import ExitStack
+
+import concourse.mybir as mybir
+from concourse.masks import make_identity
+
+F32 = mybir.dt.float32
+BF16 = mybir.dt.bfloat16
+U32 = mybir.dt.uint32
+U8 = mybir.dt.uint8
+FP8X4 = mybir.dt.float8_e4m3fn_x4
+RELU = mybir.ActivationFunctionType.Relu
+ADD = mybir.AluOpType.add
+
+P = 128
+PACK = 4
+K_PASS = P * PACK
+BANK = 512
+
+NS, ND, D0, D1 = 1024, 8192, 512, 512
+PASSES = NS // K_PASS
+
+TILES = 4
+GROUP = TILES * P
+GROUPS = ND // GROUP
+LEAD = 3
+RAW_BUFS = 8
+
+FLOPS = 2 * NS * D0 * D1 + 2 * ND * NS * D1
+
+
+def tile_gcn_pa_t_kernel(tc, x, adj, W0, b0, out):
+    nc = tc.nc
+    with ExitStack() as ctx:
+        ctx.enter_context(tc.manual_schedule())
+        const = ctx.enter_context(tc.tile_pool(name="const", bufs=1))
+        raw_pool = ctx.enter_context(tc.tile_pool(name="raw", bufs=RAW_BUFS))
+        grouped_pool = ctx.enter_context(tc.tile_pool(name="grouped", bufs=LEAD + 1))
+        mx_pool = ctx.enter_context(tc.tile_pool(name="mx", bufs=LEAD + 1))
+        out_pool = ctx.enter_context(tc.tile_pool(name="outs", bufs=4))
+        flip_psum = ctx.enter_context(tc.psum_pool(name="flip", bufs=TILES))
+        sum_psum = ctx.enter_context(tc.psum_pool(name="sums", bufs=TILES))
+
+        ident = const.tile([P, P], F32)
+        make_identity(nc, ident[:])
+        ones = const.tile([P, P], BF16)
+        nc.vector.memset(ones[:], 1.0)
+        bias_rows = const.tile([P, D1], BF16)
+        nc.vector.memset(bias_rows[:], 0.0)
+        nc.scalar.dma_start(out=bias_rows[0:1, :], in_=b0.rearrange("(o n) -> o n", o=1))
+
+        x_raw = const.tile([P, 4 * 2 * D0], BF16)
+        x_view = x.rearrange("(a p e) d -> p a (e d)", a=4, p=P, e=2)
+        x_halves = x_raw[:].rearrange("p (g a w) -> p g a w", g=PASSES, a=2)
+        w_raw = const.tile([P, PACK * D1], BF16)
+        nc.sync.dma_start(out=x_halves[:, 0], in_=x_view[:, 0:2, :])
+        nc.sync.dma_start(
+            out=w_raw[:].rearrange("p (u w) -> p u w", u=2),
+            in_=W0.rearrange("(u q e) c -> q u (e c)", u=2, q=P, e=2),
+        )
+        nc.sync.dma_start(out=x_halves[:, 1], in_=x_view[:, 2:4, :])
+
+        adj_view = adj.rearrange("(i p j) k -> i p (j k)", p=P, j=TILES)
+        out_view = out.rearrange("(i p j) n -> i p (j n)", p=P, j=TILES)
+        raw, grouped, codes, scales = {}, {}, {}, {}
+
+        def load(i):
+            adj_raw = raw_pool.tile([P, TILES * NS], BF16)
+            nc.sync.dma_start(out=adj_raw[:], in_=adj_view[i])
+            raw[i] = adj_raw
+
+        for i in range(RAW_BUFS):
+            load(i)
+
+        def flip_words(words, dest_words, engine_copy):
+            bank = flip_psum.tile([P, BANK], F32)
+            for q in range(4):
+                nc.tensor.transpose(bank[:, q * P : (q + 1) * P], words[:, q * P : (q + 1) * P], ident[:])
+            engine_copy(
+                out=dest_words.rearrange("p (s r u) -> p s r u", s=2, u=2),
+                in_=bank[:].rearrange("p (s u r) -> p s r u", s=2, u=2),
+            )
+
+        x_words = x_raw[:].bitcast(F32)
+        x_grouped = const.tile([P, 8 * K_PASS], BF16, align_bytes=64)
+        x_grouped_words = x_grouped[:].bitcast(F32)
+        x_codes = const.tile([P, NS], U32, align_bytes=64)
+        x_scales = const.tile([P, NS], U8, align_bytes=64)
+        w_grouped = const.tile([P, D1 * PACK], BF16, align_bytes=64)
+        w_codes = const.tile([P, D1], U32, align_bytes=64)
+        w_scales = const.tile([P, D1], U8, align_bytes=64)
+        bias_all = const.tile([P, D1], F32)
+        h_grouped = const.tile([P, PASSES * D1 * PACK], BF16, align_bytes=64)
+        h_codes = const.tile([P, PASSES * D1], U32, align_bytes=64)
+        h_scales = const.tile([P, PASSES * D1], U8, align_bytes=64)
+
+        def flip_x(a):
+            cols = slice(a * BANK, (a + 1) * BANK)
+            flip_words(x_words[:, cols], x_grouped_words[:, cols], nc.scalar.copy)
+
+        def quantise_x(g):
+            nc.vector.quantize_mx(
+                out=x_codes[:, g * K_PASS : (g + 1) * K_PASS].bitcast(FP8X4),
+                scales=x_scales[:, g * K_PASS : (g + 1) * K_PASS],
+                in_=x_grouped[:, g * PACK * K_PASS : (g + 1) * PACK * K_PASS],
+            )
+
+        def first_product(g):
+            for cb in range(D1 // P):
+                h_bank = sum_psum.tile([P, BANK], F32, tag="sums")
+                for t in range(PACK):
+                    nodes = slice((PACK * g + t) * P, (PACK * g + t + 1) * P)
+                    nc.tensor.matmul_mx(
+                        out=h_bank[:, t * P : (t + 1) * P],
+                        lhsT=x_codes[:, nodes].bitcast(FP8X4),
+                        lhsT_scale=x_scales[:, nodes],
+                        rhs=w_codes[:, cb * P : (cb + 1) * P].bitcast(FP8X4),
+                        rhs_scale=w_scales[:, cb * P : (cb + 1) * P],
+                        start=True,
+                        stop=True,
+                    )
+                first = (g * D1 + cb * P) * PACK
+                nc.vector.tensor_tensor(
+                    out=h_grouped[:, first : first + P * PACK].rearrange("p (c t) -> p c t", t=PACK),
+                    in0=h_bank[:].rearrange("p (t c) -> p c t", t=PACK),
+                    in1=bias_all[:, cb * P : (cb + 1) * P].unsqueeze(2).to_broadcast([P, P, PACK]),
+                    op=ADD,
+                )
+
+        def quantise_h(g):
+            nc.vector.quantize_mx(
+                out=h_codes[:, g * D1 : (g + 1) * D1].bitcast(FP8X4),
+                scales=h_scales[:, g * D1 : (g + 1) * D1],
+                in_=h_grouped[:, g * D1 * PACK : (g + 1) * D1 * PACK],
+            )
+
+        def flip_group(i):
+            adj_grouped = grouped_pool.tile([P, TILES * NS], BF16, align_bytes=64)
+            grouped[i] = adj_grouped
+            words = raw[i][:].bitcast(F32)
+            dest = adj_grouped[:].bitcast(F32)
+            for j in range(TILES):
+                by_scalar = i < LEAD or j == TILES - 1
+                cols = slice(j * BANK, (j + 1) * BANK)
+                flip_words(words[:, cols], dest[:, cols], nc.scalar.copy if by_scalar else nc.vector.tensor_copy)
+
+        def quantise_group(i):
+            adj_codes = mx_pool.tile([P, TILES * PASSES * P], U32, align_bytes=64)
+            adj_scales = mx_pool.tile([P, TILES * PASSES * P], U8, align_bytes=64)
+            nc.vector.quantize_mx(out=adj_codes[:].bitcast(FP8X4), scales=adj_scales[:], in_=grouped[i][:])
+            codes[i], scales[i] = adj_codes, adj_scales
+
+        def multiply_group(i):
+            result = out_pool.tile([P, TILES * D1], F32)
+            for j in range(TILES):
+                acc = sum_psum.tile([P, BANK], F32, tag="sums")
+                for g in range(PASSES):
+                    nodes = slice((j * PASSES + g) * P, (j * PASSES + g + 1) * P)
+                    nc.tensor.matmul_mx(
+                        out=acc[:],
+                        lhsT=codes[i][:, nodes].bitcast(FP8X4),
+                        lhsT_scale=scales[i][:, nodes],
+                        rhs=h_codes[:, g * D1 : (g + 1) * D1].bitcast(FP8X4),
+                        rhs_scale=h_scales[:, g * D1 : (g + 1) * D1],
+                        start=(g == 0),
+                        stop=(g == PASSES - 1),
+                    )
+                nc.scalar.activation(out=result[:, j * D1 : (j + 1) * D1], in_=acc[:], func=RELU)
+            nc.scalar.dma_start(out=out_view[i], in_=result[:])
+
+        flip_x(0)
+        flip_x(1)
+        bias_bank = sum_psum.tile([P, BANK], F32, tag="sums")
+        nc.tensor.matmul(bias_bank[:], lhsT=ones[:], rhs=bias_rows[:], start=True, stop=True)
+        nc.scalar.copy(out=bias_all[:], in_=bias_bank[:])
+        nc.vector.tensor_copy(
+            out=w_grouped[:].rearrange("p (c t) -> p c t", t=PACK),
+            in_=w_raw[:].rearrange("p (t c) -> p c t", t=PACK),
+        )
+        flip_x(2)
+        flip_x(3)
+        nc.vector.quantize_mx(out=w_codes[:].bitcast(FP8X4), scales=w_scales[:], in_=w_grouped[:])
+        quantise_x(0)
+        quantise_x(1)
+        first_product(0)
+        flip_group(0)
+        quantise_h(0)
+        first_product(1)
+        flip_group(1)
+        flip_group(2)
+        quantise_group(0)
+        quantise_h(1)
+        quantise_group(1)
+        for i in range(GROUPS):
+            if i + RAW_BUFS < GROUPS:
+                load(i + RAW_BUFS)
+            if i + LEAD < GROUPS:
+                flip_group(i + LEAD)
+            if i + LEAD - 1 < GROUPS:
+                quantise_group(i + LEAD - 1)
+            multiply_group(i)

@@ -22,8 +22,9 @@ PASSES = NS // K_PASS
 TILES = 4
 GROUP = TILES * P
 GROUPS = ND // GROUP
-LEAD = 3
-RAW_BUFS = 8
+LEAD = 2
+RAW_BUFS = 10
+OUT_BUFS = 5
 
 FLOPS = 2 * NS * D0 * D1 + 2 * ND * NS * D1
 
@@ -36,23 +37,23 @@ def tile_gcn_pa_t_kernel(tc, x, adj, W0, b0, out):
         raw_pool = ctx.enter_context(tc.tile_pool(name="raw", bufs=RAW_BUFS))
         grouped_pool = ctx.enter_context(tc.tile_pool(name="grouped", bufs=LEAD + 1))
         mx_pool = ctx.enter_context(tc.tile_pool(name="mx", bufs=LEAD + 1))
-        out_pool = ctx.enter_context(tc.tile_pool(name="outs", bufs=4))
+        out_pool = ctx.enter_context(tc.tile_pool(name="outs", bufs=OUT_BUFS))
         flip_psum = ctx.enter_context(tc.psum_pool(name="flip", bufs=TILES))
         sum_psum = ctx.enter_context(tc.psum_pool(name="sums", bufs=TILES))
 
         ident = const.tile([P, P], F32)
         make_identity(nc, ident[:])
-        ones = const.tile([P, P], BF16)
-        nc.vector.memset(ones[:], 1.0)
         bias_rows = const.tile([P, D1], BF16)
         nc.vector.memset(bias_rows[:], 0.0)
-        nc.scalar.dma_start(out=bias_rows[0:1, :], in_=b0.rearrange("(o n) -> o n", o=1))
+        ones = const.tile([P, P], BF16)
+        nc.vector.memset(ones[:], 1.0)
 
         x_raw = const.tile([P, 4 * 2 * D0], BF16)
         x_view = x.rearrange("(a p e) d -> p a (e d)", a=4, p=P, e=2)
         x_halves = x_raw[:].rearrange("p (g a w) -> p g a w", g=PASSES, a=2)
         w_raw = const.tile([P, PACK * D1], BF16)
         nc.sync.dma_start(out=x_halves[:, 0], in_=x_view[:, 0:2, :])
+        nc.sync.dma_start(out=bias_rows[0:1, :], in_=b0.rearrange("(o n) -> o n", o=1))
         nc.sync.dma_start(
             out=w_raw[:].rearrange("p (u w) -> p u w", u=2),
             in_=W0.rearrange("(u q e) c -> q u (e c)", u=2, q=P, e=2),
@@ -72,7 +73,7 @@ def tile_gcn_pa_t_kernel(tc, x, adj, W0, b0, out):
             load(i)
 
         def flip_words(words, dest_words, engine_copy):
-            bank = flip_psum.tile([P, BANK], F32)
+            bank = flip_psum.tile([P, BANK], F32, tag="flip")
             for q in range(4):
                 nc.tensor.transpose(bank[:, q * P : (q + 1) * P], words[:, q * P : (q + 1) * P], ident[:])
             engine_copy(
@@ -106,7 +107,10 @@ def tile_gcn_pa_t_kernel(tc, x, adj, W0, b0, out):
 
         def first_product(g):
             for cb in range(D1 // P):
-                h_bank = sum_psum.tile([P, BANK], F32, tag="sums")
+                if g == 0:
+                    h_bank = sum_psum.tile([P, BANK], F32, tag="sums")
+                else:
+                    h_bank = flip_psum.tile([P, BANK], F32, tag="flip")
                 for t in range(PACK):
                     nodes = slice((PACK * g + t) * P, (PACK * g + t + 1) * P)
                     nc.tensor.matmul_mx(
@@ -126,13 +130,6 @@ def tile_gcn_pa_t_kernel(tc, x, adj, W0, b0, out):
                     op=ADD,
                 )
 
-        def quantise_h(g):
-            nc.vector.quantize_mx(
-                out=h_codes[:, g * D1 : (g + 1) * D1].bitcast(FP8X4),
-                scales=h_scales[:, g * D1 : (g + 1) * D1],
-                in_=h_grouped[:, g * D1 * PACK : (g + 1) * D1 * PACK],
-            )
-
         def flip_group(i):
             adj_grouped = grouped_pool.tile([P, TILES * NS], BF16, align_bytes=64)
             grouped[i] = adj_grouped
@@ -151,6 +148,7 @@ def tile_gcn_pa_t_kernel(tc, x, adj, W0, b0, out):
 
         def multiply_group(i):
             result = out_pool.tile([P, TILES * D1], F32)
+            tiles_a_store = 1 if i == GROUPS - 1 else TILES
             for j in range(TILES):
                 acc = sum_psum.tile([P, BANK], F32, tag="sums")
                 for g in range(PASSES):
@@ -165,7 +163,9 @@ def tile_gcn_pa_t_kernel(tc, x, adj, W0, b0, out):
                         stop=(g == PASSES - 1),
                     )
                 nc.scalar.activation(out=result[:, j * D1 : (j + 1) * D1], in_=acc[:], func=RELU)
-            nc.scalar.dma_start(out=out_view[i], in_=result[:])
+                if (j + 1) % tiles_a_store == 0:
+                    cols = slice((j + 1 - tiles_a_store) * D1, (j + 1) * D1)
+                    nc.scalar.dma_start(out=out_view[i][:, cols], in_=result[:, cols])
 
         flip_x(0)
         flip_x(1)
@@ -182,19 +182,16 @@ def tile_gcn_pa_t_kernel(tc, x, adj, W0, b0, out):
         quantise_x(0)
         quantise_x(1)
         first_product(0)
-        flip_group(0)
-        quantise_h(0)
         first_product(1)
-        flip_group(1)
-        flip_group(2)
+        nc.vector.quantize_mx(out=h_codes[:].bitcast(FP8X4), scales=h_scales[:], in_=h_grouped[:])
+        for i in range(LEAD):
+            flip_group(i)
         quantise_group(0)
-        quantise_h(1)
-        quantise_group(1)
         for i in range(GROUPS):
             if i + RAW_BUFS < GROUPS:
                 load(i + RAW_BUFS)
+            if i + 1 < GROUPS:
+                quantise_group(i + 1)
+            multiply_group(i)
             if i + LEAD < GROUPS:
                 flip_group(i + LEAD)
-            if i + LEAD - 1 < GROUPS:
-                quantise_group(i + LEAD - 1)
-            multiply_group(i)

@@ -165,7 +165,7 @@ def tile_gcn_pa_t_kernel(tc, x, adj, W0, b0, out):
                 nc.scalar.activation(out=result[:, j * D1 : (j + 1) * D1], in_=acc[:], func=RELU)
                 if (j + 1) % tiles_a_store == 0:
                     cols = slice((j + 1 - tiles_a_store) * D1, (j + 1) * D1)
-                    nc.scalar.dma_start(out=out_view[i][:, cols], in_=result[:, cols])
+                    nc.sync.dma_start(out=out_view[i][:, cols], in_=result[:, cols])
 
         flip_x(0)
         flip_x(1)

@@ -22,9 +22,10 @@ PASSES = NS // K_PASS
 TILES = 4
 GROUP = TILES * P
 GROUPS = ND // GROUP
-LEAD = 2
-RAW_BUFS = 10
-OUT_BUFS = 5
+RUN = 2
+RUNS = GROUPS // RUN
+RAW_BUFS = 5
+OUT_BUFS = 6
 
 FLOPS = 2 * NS * D0 * D1 + 2 * ND * NS * D1
 
@@ -35,8 +36,8 @@ def tile_gcn_pa_t_kernel(tc, x, adj, W0, b0, out):
         ctx.enter_context(tc.manual_schedule())
         const = ctx.enter_context(tc.tile_pool(name="const", bufs=1))
         raw_pool = ctx.enter_context(tc.tile_pool(name="raw", bufs=RAW_BUFS))
-        grouped_pool = ctx.enter_context(tc.tile_pool(name="grouped", bufs=LEAD + 1))
-        mx_pool = ctx.enter_context(tc.tile_pool(name="mx", bufs=LEAD + 1))
+        grouped_pool = ctx.enter_context(tc.tile_pool(name="grouped", bufs=RUN + 1))
+        mx_pool = ctx.enter_context(tc.tile_pool(name="mx", bufs=RUN + 2))
         out_pool = ctx.enter_context(tc.tile_pool(name="outs", bufs=OUT_BUFS))
         flip_psum = ctx.enter_context(tc.psum_pool(name="flip", bufs=TILES))
         sum_psum = ctx.enter_context(tc.psum_pool(name="sums", bufs=TILES))
@@ -60,17 +61,17 @@ def tile_gcn_pa_t_kernel(tc, x, adj, W0, b0, out):
         )
         nc.sync.dma_start(out=x_halves[:, 1], in_=x_view[:, 2:4, :])
 
-        adj_view = adj.rearrange("(i p j) k -> i p (j k)", p=P, j=TILES)
-        out_view = out.rearrange("(i p j) n -> i p (j n)", p=P, j=TILES)
+        adj_view = adj.rearrange("(c p j) k -> c p (j k)", p=P, j=RUN * TILES)
+        out_view = out.rearrange("(c p s j) n -> c s p (j n)", p=P, s=RUN, j=TILES)
         raw, grouped, codes, scales = {}, {}, {}, {}
 
-        def load(i):
-            adj_raw = raw_pool.tile([P, TILES * NS], BF16)
-            nc.sync.dma_start(out=adj_raw[:], in_=adj_view[i])
-            raw[i] = adj_raw
+        def load(c):
+            adj_raw = raw_pool.tile([P, RUN * TILES * NS], BF16)
+            nc.sync.dma_start(out=adj_raw[:], in_=adj_view[c])
+            raw[c] = adj_raw
 
-        for i in range(RAW_BUFS):
-            load(i)
+        for c in range(RAW_BUFS):
+            load(c)
 
         def flip_words(words, dest_words, engine_copy):
             bank = flip_psum.tile([P, BANK], F32, tag="flip")
@@ -133,12 +134,16 @@ def tile_gcn_pa_t_kernel(tc, x, adj, W0, b0, out):
         def flip_group(i):
             adj_grouped = grouped_pool.tile([P, TILES * NS], BF16, align_bytes=64)
             grouped[i] = adj_grouped
-            words = raw[i][:].bitcast(F32)
+            words = raw[i // RUN][:].bitcast(F32)
             dest = adj_grouped[:].bitcast(F32)
             for j in range(TILES):
-                by_scalar = i < LEAD or j == TILES - 1
-                cols = slice(j * BANK, (j + 1) * BANK)
-                flip_words(words[:, cols], dest[:, cols], nc.scalar.copy if by_scalar else nc.vector.tensor_copy)
+                by_scalar = i < RUN or j % 2 == 1
+                tile_in_run = (i % RUN) * TILES + j
+                flip_words(
+                    words[:, tile_in_run * BANK : (tile_in_run + 1) * BANK],
+                    dest[:, j * BANK : (j + 1) * BANK],
+                    nc.scalar.copy if by_scalar else nc.vector.tensor_copy,
+                )
 
         def quantise_group(i):
             adj_codes = mx_pool.tile([P, TILES * PASSES * P], U32, align_bytes=64)
@@ -162,10 +167,13 @@ def tile_gcn_pa_t_kernel(tc, x, adj, W0, b0, out):
                         start=(g == 0),
                         stop=(g == PASSES - 1),
                     )
-                nc.scalar.activation(out=result[:, j * D1 : (j + 1) * D1], in_=acc[:], func=RELU)
+                if j == TILES - 1:
+                    nc.vector.tensor_relu(out=result[:, j * D1 : (j + 1) * D1], in_=acc[:])
+                else:
+                    nc.scalar.activation(out=result[:, j * D1 : (j + 1) * D1], in_=acc[:], func=RELU)
                 if (j + 1) % tiles_a_store == 0:
                     cols = slice((j + 1 - tiles_a_store) * D1, (j + 1) * D1)
-                    nc.sync.dma_start(out=out_view[i][:, cols], in_=result[:, cols])
+                    nc.sync.dma_start(out=out_view[i // RUN, i % RUN][:, cols], in_=result[:, cols])
 
         flip_x(0)
         flip_x(1)
@@ -184,14 +192,13 @@ def tile_gcn_pa_t_kernel(tc, x, adj, W0, b0, out):
         first_product(0)
         first_product(1)
         nc.vector.quantize_mx(out=h_codes[:].bitcast(FP8X4), scales=h_scales[:], in_=h_grouped[:])
-        for i in range(LEAD):
-            flip_group(i)
-        quantise_group(0)
-        for i in range(GROUPS):
-            if i + RAW_BUFS < GROUPS:
-                load(i + RAW_BUFS)
-            if i + 1 < GROUPS:
-                quantise_group(i + 1)
-            multiply_group(i)
-            if i + LEAD < GROUPS:
-                flip_group(i + LEAD)
+        for first in range(0, GROUPS, RUN):
+            for i in range(first, first + RUN):
+                flip_group(i)
+            if first // RUN + RAW_BUFS < RUNS:
+                load(first // RUN + RAW_BUFS)
+            for i in range(first, first + RUN):
+                quantise_group(i)
+            for i in range(max(first - 1, 0), first + RUN - 1):
+                multiply_group(i)
+        multiply_group(GROUPS - 1)

@@ -24,8 +24,9 @@ GROUP = TILES * P
 GROUPS = ND // GROUP
 RUN = 2
 RUNS = GROUPS // RUN
+AHEAD = 3
 RAW_BUFS = 5
-OUT_BUFS = 6
+OUT_BUFS = 7
 
 FLOPS = 2 * NS * D0 * D1 + 2 * ND * NS * D1
 
@@ -36,8 +37,8 @@ def tile_gcn_pa_t_kernel(tc, x, adj, W0, b0, out):
         ctx.enter_context(tc.manual_schedule())
         const = ctx.enter_context(tc.tile_pool(name="const", bufs=1))
         raw_pool = ctx.enter_context(tc.tile_pool(name="raw", bufs=RAW_BUFS))
-        grouped_pool = ctx.enter_context(tc.tile_pool(name="grouped", bufs=RUN + 1))
-        mx_pool = ctx.enter_context(tc.tile_pool(name="mx", bufs=RUN + 2))
+        grouped_pool = ctx.enter_context(tc.tile_pool(name="grouped", bufs=RUN + 2))
+        mx_pool = ctx.enter_context(tc.tile_pool(name="mx", bufs=RUN + 3))
         out_pool = ctx.enter_context(tc.tile_pool(name="outs", bufs=OUT_BUFS))
         flip_psum = ctx.enter_context(tc.psum_pool(name="flip", bufs=TILES))
         sum_psum = ctx.enter_context(tc.psum_pool(name="sums", bufs=TILES))
@@ -53,21 +54,24 @@ def tile_gcn_pa_t_kernel(tc, x, adj, W0, b0, out):
         x_view = x.rearrange("(a p e) d -> p a (e d)", a=4, p=P, e=2)
         x_halves = x_raw[:].rearrange("p (g a w) -> p g a w", g=PASSES, a=2)
         w_raw = const.tile([P, PACK * D1], BF16)
-        nc.sync.dma_start(out=x_halves[:, 0], in_=x_view[:, 0:2, :])
-        nc.sync.dma_start(out=bias_rows[0:1, :], in_=b0.rearrange("(o n) -> o n", o=1))
         nc.sync.dma_start(
             out=w_raw[:].rearrange("p (u w) -> p u w", u=2),
             in_=W0.rearrange("(u q e) c -> q u (e c)", u=2, q=P, e=2),
         )
+        nc.sync.dma_start(out=bias_rows[0:1, :], in_=b0.rearrange("(o n) -> o n", o=1))
+        nc.sync.dma_start(out=x_halves[:, 0], in_=x_view[:, 0:2, :])
         nc.sync.dma_start(out=x_halves[:, 1], in_=x_view[:, 2:4, :])
 
         adj_view = adj.rearrange("(c p j) k -> c p (j k)", p=P, j=RUN * TILES)
         out_view = out.rearrange("(c p s j) n -> c s p (j n)", p=P, s=RUN, j=TILES)
-        raw, grouped, codes, scales = {}, {}, {}, {}
+        raw, grouped, codes, scales, accs, results = {}, {}, {}, {}, {}, {}
 
         def load(c):
             adj_raw = raw_pool.tile([P, RUN * TILES * NS], BF16)
-            nc.sync.dma_start(out=adj_raw[:], in_=adj_view[c])
+            step = (TILES if c < 2 else RUN * TILES) * NS
+            for first in range(0, RUN * TILES * NS, step):
+                cols = slice(first, first + step)
+                nc.sync.dma_start(out=adj_raw[:, cols], in_=adj_view[c][:, cols])
             raw[c] = adj_raw
 
         for c in range(RAW_BUFS):
@@ -83,7 +87,7 @@ def tile_gcn_pa_t_kernel(tc, x, adj, W0, b0, out):
             )
 
         x_words = x_raw[:].bitcast(F32)
-        x_grouped = const.tile([P, 8 * K_PASS], BF16, align_bytes=64)
+        x_grouped = grouped_pool.tile([P, TILES * NS], BF16, tag="grouped", align_bytes=64)
         x_grouped_words = x_grouped[:].bitcast(F32)
         x_codes = const.tile([P, NS], U32, align_bytes=64)
         x_scales = const.tile([P, NS], U8, align_bytes=64)
@@ -91,13 +95,14 @@ def tile_gcn_pa_t_kernel(tc, x, adj, W0, b0, out):
         w_codes = const.tile([P, D1], U32, align_bytes=64)
         w_scales = const.tile([P, D1], U8, align_bytes=64)
         bias_all = const.tile([P, D1], F32)
-        h_grouped = const.tile([P, PASSES * D1 * PACK], BF16, align_bytes=64)
+        h_grouped = grouped_pool.tile([P, TILES * NS], BF16, tag="grouped", align_bytes=64)
         h_codes = const.tile([P, PASSES * D1], U32, align_bytes=64)
         h_scales = const.tile([P, PASSES * D1], U8, align_bytes=64)
 
         def flip_x(a):
             cols = slice(a * BANK, (a + 1) * BANK)
-            flip_words(x_words[:, cols], x_grouped_words[:, cols], nc.scalar.copy)
+            engine_copy = nc.vector.tensor_copy if a == 1 else nc.scalar.copy
+            flip_words(x_words[:, cols], x_grouped_words[:, cols], engine_copy)
 
         def quantise_x(g):
             nc.vector.quantize_mx(
@@ -106,99 +111,178 @@ def tile_gcn_pa_t_kernel(tc, x, adj, W0, b0, out):
                 in_=x_grouped[:, g * PACK * K_PASS : (g + 1) * PACK * K_PASS],
             )
 
-        def first_product(g):
-            for cb in range(D1 // P):
-                if g == 0:
-                    h_bank = sum_psum.tile([P, BANK], F32, tag="sums")
-                else:
-                    h_bank = flip_psum.tile([P, BANK], F32, tag="flip")
-                for t in range(PACK):
-                    nodes = slice((PACK * g + t) * P, (PACK * g + t + 1) * P)
-                    nc.tensor.matmul_mx(
-                        out=h_bank[:, t * P : (t + 1) * P],
-                        lhsT=x_codes[:, nodes].bitcast(FP8X4),
-                        lhsT_scale=x_scales[:, nodes],
-                        rhs=w_codes[:, cb * P : (cb + 1) * P].bitcast(FP8X4),
-                        rhs_scale=w_scales[:, cb * P : (cb + 1) * P],
-                        start=True,
-                        stop=True,
-                    )
-                first = (g * D1 + cb * P) * PACK
-                nc.vector.tensor_tensor(
-                    out=h_grouped[:, first : first + P * PACK].rearrange("p (c t) -> p c t", t=PACK),
-                    in0=h_bank[:].rearrange("p (t c) -> p c t", t=PACK),
-                    in1=bias_all[:, cb * P : (cb + 1) * P].unsqueeze(2).to_broadcast([P, P, PACK]),
-                    op=ADD,
+        def group_w(half):
+            cols = slice(half * D1 // 2, (half + 1) * D1 // 2)
+            nc.vector.tensor_copy(
+                out=w_grouped[:].rearrange("p (c t) -> p c t", t=PACK)[:, cols, :],
+                in_=w_raw[:].rearrange("p (t c) -> p c t", t=PACK)[:, cols, :],
+            )
+
+        def quantise_w(half):
+            cols = slice(half * D1 // 2, (half + 1) * D1 // 2)
+            nc.vector.quantize_mx(
+                out=w_codes[:, cols].bitcast(FP8X4),
+                scales=w_scales[:, cols],
+                in_=w_grouped[:, half * D1 * PACK // 2 : (half + 1) * D1 * PACK // 2],
+            )
+
+        h_banks = {}
+
+        def first_product(g, cb):
+            h_bank = sum_psum.tile([P, BANK], F32, tag="sums")
+            h_banks[g, cb] = h_bank
+            for t in range(PACK):
+                nodes = slice((PACK * g + t) * P, (PACK * g + t + 1) * P)
+                nc.tensor.matmul_mx(
+                    out=h_bank[:, t * P : (t + 1) * P],
+                    lhsT=x_codes[:, nodes].bitcast(FP8X4),
+                    lhsT_scale=x_scales[:, nodes],
+                    rhs=w_codes[:, cb * P : (cb + 1) * P].bitcast(FP8X4),
+                    rhs_scale=w_scales[:, cb * P : (cb + 1) * P],
+                    start=True,
+                    stop=True,
                 )
+
+        def add_bias(g, cb):
+            first = (g * D1 + cb * P) * PACK
+            nc.vector.tensor_tensor(
+                out=h_grouped[:, first : first + P * PACK].rearrange("p (c t) -> p c t", t=PACK),
+                in0=h_banks[g, cb][:].rearrange("p (t c) -> p c t", t=PACK),
+                in1=bias_all[:, cb * P : (cb + 1) * P].unsqueeze(2).to_broadcast([P, P, PACK]),
+                op=ADD,
+            )
+
+        def quantise_h(g):
+            nc.vector.quantize_mx(
+                out=h_codes[:, g * D1 : (g + 1) * D1].bitcast(FP8X4),
+                scales=h_scales[:, g * D1 : (g + 1) * D1],
+                in_=h_grouped[:, g * D1 * PACK : (g + 1) * D1 * PACK],
+            )
+
+        def flip_tile(i, j):
+            if j == 0:
+                adj_grouped = grouped_pool.tile([P, TILES * NS], BF16, tag="grouped", align_bytes=64)
+                grouped[i] = adj_grouped
+            words = raw[i // RUN][:].bitcast(F32)
+            dest = grouped[i][:].bitcast(F32)
+            by_scalar = i < AHEAD or j % 2 == 1
+            tile_in_run = (i % RUN) * TILES + j
+            flip_words(
+                words[:, tile_in_run * BANK : (tile_in_run + 1) * BANK],
+                dest[:, j * BANK : (j + 1) * BANK],
+                nc.scalar.copy if by_scalar else nc.vector.tensor_copy,
+            )
 
         def flip_group(i):
-            adj_grouped = grouped_pool.tile([P, TILES * NS], BF16, align_bytes=64)
-            grouped[i] = adj_grouped
-            words = raw[i // RUN][:].bitcast(F32)
-            dest = adj_grouped[:].bitcast(F32)
             for j in range(TILES):
-                by_scalar = i < RUN or j % 2 == 1
-                tile_in_run = (i % RUN) * TILES + j
-                flip_words(
-                    words[:, tile_in_run * BANK : (tile_in_run + 1) * BANK],
-                    dest[:, j * BANK : (j + 1) * BANK],
-                    nc.scalar.copy if by_scalar else nc.vector.tensor_copy,
-                )
+                flip_tile(i, j)
+            if i % RUN == RUN - 1 and i // RUN + RAW_BUFS < RUNS:
+                load(i // RUN + RAW_BUFS)
 
-        def quantise_group(i):
-            adj_codes = mx_pool.tile([P, TILES * PASSES * P], U32, align_bytes=64)
-            adj_scales = mx_pool.tile([P, TILES * PASSES * P], U8, align_bytes=64)
-            nc.vector.quantize_mx(out=adj_codes[:].bitcast(FP8X4), scales=adj_scales[:], in_=grouped[i][:])
-            codes[i], scales[i] = adj_codes, adj_scales
+        def quantise_tiles(i, first, count):
+            if first == 0:
+                adj_codes = mx_pool.tile([P, TILES * PASSES * P], U32, align_bytes=64)
+                adj_scales = mx_pool.tile([P, TILES * PASSES * P], U8, align_bytes=64)
+                codes[i], scales[i] = adj_codes, adj_scales
+            cols = slice(first * PASSES * P, (first + count) * PASSES * P)
+            nc.vector.quantize_mx(
+                out=codes[i][:, cols].bitcast(FP8X4),
+                scales=scales[i][:, cols],
+                in_=grouped[i][:, first * NS : (first + count) * NS],
+            )
+
+        def multiply(i, j, g):
+            if g == 0:
+                acc = sum_psum.tile([P, BANK], F32, tag="sums")
+                accs[i, j] = acc
+            nodes = slice((j * PASSES + g) * P, (j * PASSES + g + 1) * P)
+            nc.tensor.matmul_mx(
+                out=accs[i, j][:],
+                lhsT=codes[i][:, nodes].bitcast(FP8X4),
+                lhsT_scale=scales[i][:, nodes],
+                rhs=h_codes[:, g * D1 : (g + 1) * D1].bitcast(FP8X4),
+                rhs_scale=h_scales[:, g * D1 : (g + 1) * D1],
+                start=(g == 0),
+                stop=(g == PASSES - 1),
+            )
+
+        def finish(i, j):
+            if j == 0:
+                result = out_pool.tile([P, TILES * D1], F32)
+                results[i] = result
+            cols = slice(j * D1, (j + 1) * D1)
+            if j == TILES - 1:
+                nc.vector.tensor_relu(out=results[i][:, cols], in_=accs[i, j][:])
+            else:
+                nc.scalar.activation(out=results[i][:, cols], in_=accs[i, j][:], func=RELU)
+            tiles_a_store = 1 if i == GROUPS - 1 else TILES
+            if (j + 1) % tiles_a_store == 0:
+                cols = slice((j + 1 - tiles_a_store) * D1, (j + 1) * D1)
+                nc.sync.dma_start(out=out_view[i // RUN, i % RUN][:, cols], in_=results[i][:, cols])
 
         def multiply_group(i):
-            result = out_pool.tile([P, TILES * D1], F32)
-            tiles_a_store = 1 if i == GROUPS - 1 else TILES
             for j in range(TILES):
-                acc = sum_psum.tile([P, BANK], F32, tag="sums")
                 for g in range(PASSES):
-                    nodes = slice((j * PASSES + g) * P, (j * PASSES + g + 1) * P)
-                    nc.tensor.matmul_mx(
-                        out=acc[:],
-                        lhsT=codes[i][:, nodes].bitcast(FP8X4),
-                        lhsT_scale=scales[i][:, nodes],
-                        rhs=h_codes[:, g * D1 : (g + 1) * D1].bitcast(FP8X4),
-                        rhs_scale=h_scales[:, g * D1 : (g + 1) * D1],
-                        start=(g == 0),
-                        stop=(g == PASSES - 1),
-                    )
-                if j == TILES - 1:
-                    nc.vector.tensor_relu(out=result[:, j * D1 : (j + 1) * D1], in_=acc[:])
-                else:
-                    nc.scalar.activation(out=result[:, j * D1 : (j + 1) * D1], in_=acc[:], func=RELU)
-                if (j + 1) % tiles_a_store == 0:
-                    cols = slice((j + 1 - tiles_a_store) * D1, (j + 1) * D1)
-                    nc.sync.dma_start(out=out_view[i // RUN, i % RUN][:, cols], in_=result[:, cols])
+                    multiply(i, j, g)
+                finish(i, j)
 
-        flip_x(0)
-        flip_x(1)
+        group_w(0)
+        group_w(1)
         bias_bank = sum_psum.tile([P, BANK], F32, tag="sums")
         nc.tensor.matmul(bias_bank[:], lhsT=ones[:], rhs=bias_rows[:], start=True, stop=True)
         nc.scalar.copy(out=bias_all[:], in_=bias_bank[:])
-        nc.vector.tensor_copy(
-            out=w_grouped[:].rearrange("p (c t) -> p c t", t=PACK),
-            in_=w_raw[:].rearrange("p (t c) -> p c t", t=PACK),
-        )
-        flip_x(2)
-        flip_x(3)
-        nc.vector.quantize_mx(out=w_codes[:].bitcast(FP8X4), scales=w_scales[:], in_=w_grouped[:])
+        quantise_w(0)
+        quantise_w(1)
+        for a in range(PACK):
+            flip_x(a)
         quantise_x(0)
+        for cb in range(D1 // P):
+            first_product(0, cb)
+        add_bias(0, 0)
         quantise_x(1)
-        first_product(0)
-        first_product(1)
-        nc.vector.quantize_mx(out=h_codes[:].bitcast(FP8X4), scales=h_scales[:], in_=h_grouped[:])
-        for first in range(0, GROUPS, RUN):
-            for i in range(first, first + RUN):
+        add_bias(0, 1)
+        flip_tile(0, 0)
+        flip_tile(0, 1)
+        first_product(1, 0)
+        first_product(1, 1)
+        add_bias(0, 2)
+        add_bias(0, 3)
+        flip_tile(0, 2)
+        flip_tile(0, 3)
+        first_product(1, 2)
+        first_product(1, 3)
+        add_bias(1, 0)
+        quantise_h(0)
+        add_bias(1, 1)
+        flip_group(1)
+        quantise_tiles(0, 0, 2)
+        add_bias(1, 2)
+        add_bias(1, 3)
+        flip_tile(2, 0)
+        flip_tile(2, 1)
+        quantise_tiles(0, 2, 2)
+        quantise_h(1)
+        for j in range(TILES):
+            multiply(0, j, 0)
+        flip_tile(2, 2)
+        flip_tile(2, 3)
+        quantise_tiles(1, 0, TILES)
+        for j in range(TILES):
+            multiply(0, j, 1)
+            finish(0, j)
+        quantise_tiles(2, 0, TILES)
+        multiply_group(1)
+        done = AHEAD
+        for first in range(RUN, GROUPS, RUN):
+            upto = done
+            if done < GROUPS:
+                upto = GROUPS if GROUPS - done <= AHEAD else done + RUN
+            for i in range(done, upto):
                 flip_group(i)
-            if first // RUN + RAW_BUFS < RUNS:
-                load(first // RUN + RAW_BUFS)
-            for i in range(first, first + RUN):
-                quantise_group(i)
-            for i in range(max(first - 1, 0), first + RUN - 1):
-                multiply_group(i)
-        multiply_group(GROUPS - 1)
+            for step in range(RUN):
+                if done + step < upto:
+                    quantise_tiles(done + step, 0, TILES)
+                multiply_group(first + step)
+            for i in range(done + RUN, upto):
+                quantise_tiles(i, 0, TILES)
+            done = upto

@@ -211,7 +211,7 @@ def tile_gcn_pa_t_kernel(tc, x, adj, W0, b0, out):
                 result = out_pool.tile([P, TILES * D1], F32)
                 results[i] = result
             cols = slice(j * D1, (j + 1) * D1)
-            if j == TILES - 1:
+            if j == TILES - 2:
                 nc.vector.tensor_relu(out=results[i][:, cols], in_=accs[i, j][:])
             else:
                 nc.scalar.activation(out=results[i][:, cols], in_=accs[i, j][:], func=RELU)

@@ -54,12 +54,12 @@ def tile_gcn_pa_t_kernel(tc, x, adj, W0, b0, out):
         x_view = x.rearrange("(a p e) d -> p a (e d)", a=4, p=P, e=2)
         x_halves = x_raw[:].rearrange("p (g a w) -> p g a w", g=PASSES, a=2)
         w_raw = const.tile([P, PACK * D1], BF16)
+        nc.sync.dma_start(out=x_halves[:, 0], in_=x_view[:, 0:2, :])
+        nc.sync.dma_start(out=bias_rows[0:1, :], in_=b0.rearrange("(o n) -> o n", o=1))
         nc.sync.dma_start(
             out=w_raw[:].rearrange("p (u w) -> p u w", u=2),
             in_=W0.rearrange("(u q e) c -> q u (e c)", u=2, q=P, e=2),
         )
-        nc.sync.dma_start(out=bias_rows[0:1, :], in_=b0.rearrange("(o n) -> o n", o=1))
-        nc.sync.dma_start(out=x_halves[:, 0], in_=x_view[:, 0:2, :])
         nc.sync.dma_start(out=x_halves[:, 1], in_=x_view[:, 2:4, :])
 
         adj_view = adj.rearrange("(c p j) k -> c p (j k)", p=P, j=RUN * TILES)
@@ -101,8 +101,7 @@ def tile_gcn_pa_t_kernel(tc, x, adj, W0, b0, out):
 
         def flip_x(a):
             cols = slice(a * BANK, (a + 1) * BANK)
-            engine_copy = nc.vector.tensor_copy if a == 1 else nc.scalar.copy
-            flip_words(x_words[:, cols], x_grouped_words[:, cols], engine_copy)
+            flip_words(x_words[:, cols], x_grouped_words[:, cols], nc.scalar.copy)
 
         def quantise_x(g):
             nc.vector.quantize_mx(
@@ -226,21 +225,25 @@ def tile_gcn_pa_t_kernel(tc, x, adj, W0, b0, out):
                     multiply(i, j, g)
                 finish(i, j)
 
-        group_w(0)
-        group_w(1)
+        flip_x(0)
+        flip_x(1)
         bias_bank = sum_psum.tile([P, BANK], F32, tag="sums")
         nc.tensor.matmul(bias_bank[:], lhsT=ones[:], rhs=bias_rows[:], start=True, stop=True)
         nc.scalar.copy(out=bias_all[:], in_=bias_bank[:])
+        flip_x(2)
+        flip_x(3)
+        group_w(0)
         quantise_w(0)
-        quantise_w(1)
-        for a in range(PACK):
-            flip_x(a)
         quantise_x(0)
-        for cb in range(D1 // P):
-            first_product(0, cb)
+        first_product(0, 0)
+        first_product(0, 1)
+        group_w(1)
+        quantise_w(1)
+        first_product(0, 2)
+        first_product(0, 3)
         add_bias(0, 0)
-        quantise_x(1)
         add_bias(0, 1)
+        quantise_x(1)
         flip_tile(0, 0)
         flip_tile(0, 1)
         first_product(1, 0)
@@ -258,15 +261,13 @@ def tile_gcn_pa_t_kernel(tc, x, adj, W0, b0, out):
         quantise_tiles(0, 0, 2)
         add_bias(1, 2)
         add_bias(1, 3)
-        flip_tile(2, 0)
-        flip_tile(2, 1)
+        flip_group(2)
         quantise_tiles(0, 2, 2)
         quantise_h(1)
         for j in range(TILES):
             multiply(0, j, 0)
-        flip_tile(2, 2)
-        flip_tile(2, 3)
-        quantise_tiles(1, 0, TILES)
+        quantise_tiles(1, 0, 2)
+        quantise_tiles(1, 2, 2)
         for j in range(TILES):
             multiply(0, j, 1)
             finish(0, j)

@@ -26,7 +26,7 @@ RUN = 2
 RUNS = GROUPS // RUN
 AHEAD = 3
 RAW_BUFS = 5
-OUT_BUFS = 7
+OUT_BUFS = 8
 
 FLOPS = 2 * NS * D0 * D1 + 2 * ND * NS * D1
 
@@ -214,10 +214,19 @@ def tile_gcn_pa_t_kernel(tc, x, adj, W0, b0, out):
                 nc.vector.tensor_relu(out=results[i][:, cols], in_=accs[i, j][:])
             else:
                 nc.scalar.activation(out=results[i][:, cols], in_=accs[i, j][:], func=RELU)
+            ready.append((i, j))
+            if len(raw) == RUNS:
+                for tile in ready:
+                    store(*tile)
+                ready.clear()
+
+        def store(i, j):
             tiles_a_store = 1 if i == GROUPS - 1 else TILES
             if (j + 1) % tiles_a_store == 0:
                 cols = slice((j + 1 - tiles_a_store) * D1, (j + 1) * D1)
                 nc.sync.dma_start(out=out_view[i // RUN, i % RUN][:, cols], in_=results[i][:, cols])
+
+        ready = []
 
         def multiply_group(i):
             for j in range(TILES):

@@ -26,7 +26,8 @@ RUN = 2
 RUNS = GROUPS // RUN
 AHEAD = 3
 RAW_BUFS = 5
-OUT_BUFS = 8
+WHOLE_RUNS = 5
+OUT_BUFS = 4
 
 FLOPS = 2 * NS * D0 * D1 + 2 * ND * NS * D1
 
@@ -63,7 +64,7 @@ def tile_gcn_pa_t_kernel(tc, x, adj, W0, b0, out):
         nc.sync.dma_start(out=x_halves[:, 1], in_=x_view[:, 2:4, :])
 
         adj_view = adj.rearrange("(c p j) k -> c p (j k)", p=P, j=RUN * TILES)
-        out_view = out.rearrange("(c p s j) n -> c s p (j n)", p=P, s=RUN, j=TILES)
+        out_view = out.rearrange("(c p j) n -> c p (j n)", p=P, j=RUN * TILES)
         raw, grouped, codes, scales, accs, results = {}, {}, {}, {}, {}, {}
 
         def load(c):
@@ -206,25 +207,31 @@ def tile_gcn_pa_t_kernel(tc, x, adj, W0, b0, out):
             )
 
         def finish(i, j):
-            if j == 0:
-                result = out_pool.tile([P, TILES * D1], F32)
-                results[i] = result
-            cols = slice(j * D1, (j + 1) * D1)
+            tile_in_run = (i % RUN) * TILES + j
+            if tile_in_run == 0:
+                result = out_pool.tile([P, RUN * TILES * D1], F32)
+                results[i // RUN] = result
+            cols = slice(tile_in_run * D1, (tile_in_run + 1) * D1)
             if j == TILES - 2:
-                nc.vector.tensor_relu(out=results[i][:, cols], in_=accs[i, j][:])
+                nc.vector.tensor_relu(out=results[i // RUN][:, cols], in_=accs[i, j][:])
             else:
-                nc.scalar.activation(out=results[i][:, cols], in_=accs[i, j][:], func=RELU)
-            ready.append((i, j))
+                nc.scalar.activation(out=results[i // RUN][:, cols], in_=accs[i, j][:], func=RELU)
+            ready.append((i // RUN, tile_in_run + 1))
             if len(raw) == RUNS:
-                for tile in ready:
-                    store(*tile)
+                for run, tiles in ready:
+                    store(run, tiles)
                 ready.clear()
 
-        def store(i, j):
-            tiles_a_store = 1 if i == GROUPS - 1 else TILES
-            if (j + 1) % tiles_a_store == 0:
-                cols = slice((j + 1 - tiles_a_store) * D1, (j + 1) * D1)
-                nc.sync.dma_start(out=out_view[i // RUN, i % RUN][:, cols], in_=results[i][:, cols])
+        def store(run, tiles):
+            if run < WHOLE_RUNS:
+                piece = RUN * TILES
+            elif run < RUNS - 1 or tiles <= TILES:
+                piece = TILES
+            else:
+                piece = TILES // 2
+            if tiles % piece == 0:
+                cols = slice((tiles - piece) * D1, tiles * D1)
+                nc.sync.dma_start(out=out_view[run][:, cols], in_=results[run][:, cols])
 
         ready = []
 

@@ -24,6 +24,7 @@ GROUP = TILES * P
 GROUPS = ND // GROUP
 RUN = 2
 RUNS = GROUPS // RUN
+FLIP_RUN = 4
 AHEAD = 3
 RAW_BUFS = 5
 WHOLE_RUNS = 5
@@ -38,7 +39,7 @@ def tile_gcn_pa_t_kernel(tc, x, adj, W0, b0, out):
         ctx.enter_context(tc.manual_schedule())
         const = ctx.enter_context(tc.tile_pool(name="const", bufs=1))
         raw_pool = ctx.enter_context(tc.tile_pool(name="raw", bufs=RAW_BUFS))
-        grouped_pool = ctx.enter_context(tc.tile_pool(name="grouped", bufs=RUN + 2))
+        grouped_pool = ctx.enter_context(tc.tile_pool(name="grouped", bufs=FLIP_RUN + 1))
         mx_pool = ctx.enter_context(tc.tile_pool(name="mx", bufs=RUN + 3))
         out_pool = ctx.enter_context(tc.tile_pool(name="outs", bufs=OUT_BUFS))
         flip_psum = ctx.enter_context(tc.psum_pool(name="flip", bufs=TILES))
@@ -51,14 +52,15 @@ def tile_gcn_pa_t_kernel(tc, x, adj, W0, b0, out):
         ones = const.tile([P, P], BF16)
         nc.vector.memset(ones[:], 1.0)
 
-        x_raw = const.tile([P, 4 * 2 * D0], BF16)
+        head_raw = raw_pool.tile([P, RUN * TILES * NS], BF16, tag="raw")
+        x_raw = head_raw[:, 0 : 4 * 2 * D0]
         x_view = x.rearrange("(a p e) d -> p a (e d)", a=4, p=P, e=2)
-        x_halves = x_raw[:].rearrange("p (g a w) -> p g a w", g=PASSES, a=2)
-        w_raw = const.tile([P, PACK * D1], BF16)
+        x_halves = x_raw.rearrange("p (g a w) -> p g a w", g=PASSES, a=2)
+        w_raw = head_raw[:, 4 * 2 * D0 : 4 * 2 * D0 + PACK * D1]
         nc.sync.dma_start(out=x_halves[:, 0], in_=x_view[:, 0:2, :])
         nc.sync.dma_start(out=bias_rows[0:1, :], in_=b0.rearrange("(o n) -> o n", o=1))
         nc.sync.dma_start(
-            out=w_raw[:].rearrange("p (u w) -> p u w", u=2),
+            out=w_raw.rearrange("p (u w) -> p u w", u=2),
             in_=W0.rearrange("(u q e) c -> q u (e c)", u=2, q=P, e=2),
         )
         nc.sync.dma_start(out=x_halves[:, 1], in_=x_view[:, 2:4, :])
@@ -68,14 +70,14 @@ def tile_gcn_pa_t_kernel(tc, x, adj, W0, b0, out):
         raw, grouped, codes, scales, accs, results = {}, {}, {}, {}, {}, {}
 
         def load(c):
-            adj_raw = raw_pool.tile([P, RUN * TILES * NS], BF16)
+            adj_raw = raw_pool.tile([P, RUN * TILES * NS], BF16, tag="raw")
             step = (TILES if c < 2 else RUN * TILES) * NS
             for first in range(0, RUN * TILES * NS, step):
                 cols = slice(first, first + step)
                 nc.sync.dma_start(out=adj_raw[:, cols], in_=adj_view[c][:, cols])
             raw[c] = adj_raw
 
-        for c in range(RAW_BUFS):
+        for c in range(RAW_BUFS - 1):
             load(c)
 
         def flip_words(words, dest_words, engine_copy):
@@ -87,7 +89,7 @@ def tile_gcn_pa_t_kernel(tc, x, adj, W0, b0, out):
                 in_=bank[:].rearrange("p (s u r) -> p s r u", s=2, u=2),
             )
 
-        x_words = x_raw[:].bitcast(F32)
+        x_words = x_raw.bitcast(F32)
         x_grouped = grouped_pool.tile([P, TILES * NS], BF16, tag="grouped", align_bytes=64)
         x_grouped_words = x_grouped[:].bitcast(F32)
         x_codes = const.tile([P, NS], U32, align_bytes=64)
@@ -115,7 +117,7 @@ def tile_gcn_pa_t_kernel(tc, x, adj, W0, b0, out):
             cols = slice(half * D1 // 2, (half + 1) * D1 // 2)
             nc.vector.tensor_copy(
                 out=w_grouped[:].rearrange("p (c t) -> p c t", t=PACK)[:, cols, :],
-                in_=w_raw[:].rearrange("p (t c) -> p c t", t=PACK)[:, cols, :],
+                in_=w_raw.rearrange("p (t c) -> p c t", t=PACK)[:, cols, :],
             )
 
         def quantise_w(half):
@@ -254,6 +256,7 @@ def tile_gcn_pa_t_kernel(tc, x, adj, W0, b0, out):
         first_product(0, 0)
         first_product(0, 1)
         group_w(1)
+        load(RAW_BUFS - 1)
         quantise_w(1)
         first_product(0, 2)
         first_product(0, 3)
@@ -289,17 +292,13 @@ def tile_gcn_pa_t_kernel(tc, x, adj, W0, b0, out):
             finish(0, j)
         quantise_tiles(2, 0, TILES)
         multiply_group(1)
-        done = AHEAD
-        for first in range(RUN, GROUPS, RUN):
-            upto = done
-            if done < GROUPS:
-                upto = GROUPS if GROUPS - done <= AHEAD else done + RUN
+        done, first = AHEAD, RUN
+        while first < GROUPS:
+            upto = GROUPS if GROUPS - done <= FLIP_RUN + 1 else done + FLIP_RUN
             for i in range(done, upto):
                 flip_group(i)
-            for step in range(RUN):
-                if done + step < upto:
-                    quantise_tiles(done + step, 0, TILES)
-                multiply_group(first + step)
-            for i in range(done + RUN, upto):
-                quantise_tiles(i, 0, TILES)
-            done = upto
+            for i in range(first, GROUPS if upto == GROUPS else upto - 1):
+                if i + 1 < upto:
+                    quantise_tiles(i + 1, 0, TILES)
+                multiply_group(i)
+            done, first = upto, GROUPS if upto == GROUPS else upto - 1

@@ -22,11 +22,13 @@ PASSES = NS // K_PASS
 TILES = 4
 GROUP = TILES * P
 GROUPS = ND // GROUP
+LOAD = 4
+LOADS = GROUPS // LOAD
 RUN = 2
 RUNS = GROUPS // RUN
-FLIP_RUN = 4
+FLIP_RUN = 3
 AHEAD = 3
-RAW_BUFS = 5
+RAW_BUFS = 3
 WHOLE_RUNS = 5
 OUT_BUFS = 4
 
@@ -40,7 +42,7 @@ def tile_gcn_pa_t_kernel(tc, x, adj, W0, b0, out):
         const = ctx.enter_context(tc.tile_pool(name="const", bufs=1))
         raw_pool = ctx.enter_context(tc.tile_pool(name="raw", bufs=RAW_BUFS))
         grouped_pool = ctx.enter_context(tc.tile_pool(name="grouped", bufs=FLIP_RUN + 1))
-        mx_pool = ctx.enter_context(tc.tile_pool(name="mx", bufs=RUN + 3))
+        mx_pool = ctx.enter_context(tc.tile_pool(name="mx", bufs=5))
         out_pool = ctx.enter_context(tc.tile_pool(name="outs", bufs=OUT_BUFS))
         flip_psum = ctx.enter_context(tc.psum_pool(name="flip", bufs=TILES))
         sum_psum = ctx.enter_context(tc.psum_pool(name="sums", bufs=TILES))
@@ -52,7 +54,8 @@ def tile_gcn_pa_t_kernel(tc, x, adj, W0, b0, out):
         ones = const.tile([P, P], BF16)
         nc.vector.memset(ones[:], 1.0)
 
-        head_raw = raw_pool.tile([P, RUN * TILES * NS], BF16, tag="raw")
+        head_tile = out_pool.tile([P, RUN * TILES * D1], F32, tag="outs")
+        head_raw = head_tile[:].bitcast(BF16)
         x_raw = head_raw[:, 0 : 4 * 2 * D0]
         x_view = x.rearrange("(a p e) d -> p a (e d)", a=4, p=P, e=2)
         x_halves = x_raw.rearrange("p (g a w) -> p g a w", g=PASSES, a=2)
@@ -65,19 +68,19 @@ def tile_gcn_pa_t_kernel(tc, x, adj, W0, b0, out):
         )
         nc.sync.dma_start(out=x_halves[:, 1], in_=x_view[:, 2:4, :])
 
-        adj_view = adj.rearrange("(c p j) k -> c p (j k)", p=P, j=RUN * TILES)
-        out_view = out.rearrange("(c p j) n -> c p (j n)", p=P, j=RUN * TILES)
+        adj_view = adj.rearrange("(c p j) k -> c p (j k)", p=P, j=LOAD * TILES)
+        out_view = out.rearrange("(c p r j) n -> c r p (j n)", p=P, r=LOAD // RUN, j=RUN * TILES)
         raw, grouped, codes, scales, accs, results = {}, {}, {}, {}, {}, {}
 
         def load(c):
-            adj_raw = raw_pool.tile([P, RUN * TILES * NS], BF16, tag="raw")
-            step = (TILES if c < 2 else RUN * TILES) * NS
-            for first in range(0, RUN * TILES * NS, step):
+            adj_raw = raw_pool.tile([P, LOAD * TILES * NS], BF16, tag="raw")
+            step = min(1 << c, LOAD) * TILES * NS
+            for first in range(0, LOAD * TILES * NS, step):
                 cols = slice(first, first + step)
                 nc.sync.dma_start(out=adj_raw[:, cols], in_=adj_view[c][:, cols])
             raw[c] = adj_raw
 
-        for c in range(RAW_BUFS - 1):
+        for c in range(RAW_BUFS):
             load(c)
 
         def flip_words(words, dest_words, engine_copy):
@@ -165,12 +168,12 @@ def tile_gcn_pa_t_kernel(tc, x, adj, W0, b0, out):
             if j == 0:
                 adj_grouped = grouped_pool.tile([P, TILES * NS], BF16, tag="grouped", align_bytes=64)
                 grouped[i] = adj_grouped
-            words = raw[i // RUN][:].bitcast(F32)
+            words = raw[i // LOAD][:].bitcast(F32)
             dest = grouped[i][:].bitcast(F32)
             by_scalar = i < AHEAD or j % 2 == 1
-            tile_in_run = (i % RUN) * TILES + j
+            tile_in_load = (i % LOAD) * TILES + j
             flip_words(
-                words[:, tile_in_run * BANK : (tile_in_run + 1) * BANK],
+                words[:, tile_in_load * BANK : (tile_in_load + 1) * BANK],
                 dest[:, j * BANK : (j + 1) * BANK],
                 nc.scalar.copy if by_scalar else nc.vector.tensor_copy,
             )
@@ -178,8 +181,8 @@ def tile_gcn_pa_t_kernel(tc, x, adj, W0, b0, out):
         def flip_group(i):
             for j in range(TILES):
                 flip_tile(i, j)
-            if i % RUN == RUN - 1 and i // RUN + RAW_BUFS < RUNS:
-                load(i // RUN + RAW_BUFS)
+            if i % LOAD == LOAD - 1 and i // LOAD + RAW_BUFS < LOADS:
+                load(i // LOAD + RAW_BUFS)
 
         def quantise_tiles(i, first, count):
             if first == 0:
@@ -211,7 +214,7 @@ def tile_gcn_pa_t_kernel(tc, x, adj, W0, b0, out):
         def finish(i, j):
             tile_in_run = (i % RUN) * TILES + j
             if tile_in_run == 0:
-                result = out_pool.tile([P, RUN * TILES * D1], F32)
+                result = out_pool.tile([P, RUN * TILES * D1], F32, tag="outs")
                 results[i // RUN] = result
             cols = slice(tile_in_run * D1, (tile_in_run + 1) * D1)
             if j == TILES - 2:
@@ -219,7 +222,7 @@ def tile_gcn_pa_t_kernel(tc, x, adj, W0, b0, out):
             else:
                 nc.scalar.activation(out=results[i // RUN][:, cols], in_=accs[i, j][:], func=RELU)
             ready.append((i // RUN, tile_in_run + 1))
-            if len(raw) == RUNS:
+            if len(raw) == LOADS:
                 for run, tiles in ready:
                     store(run, tiles)
                 ready.clear()
@@ -233,7 +236,7 @@ def tile_gcn_pa_t_kernel(tc, x, adj, W0, b0, out):
                 piece = TILES // 2
             if tiles % piece == 0:
                 cols = slice((tiles - piece) * D1, tiles * D1)
-                nc.sync.dma_start(out=out_view[run][:, cols], in_=results[run][:, cols])
+                nc.sync.dma_start(out=out_view[run * RUN // LOAD, run % (LOAD // RUN)][:, cols], in_=results[run][:, cols])
 
         ready = []
 
@@ -256,7 +259,6 @@ def tile_gcn_pa_t_kernel(tc, x, adj, W0, b0, out):
         first_product(0, 0)
         first_product(0, 1)
         group_w(1)
-        load(RAW_BUFS - 1)
         quantise_w(1)
         first_product(0, 2)
         first_product(0, 3)

from contextlib import ExitStack

import concourse.mybir as mybir
from concourse.masks import make_identity

F32 = mybir.dt.float32
BF16 = mybir.dt.bfloat16
U32 = mybir.dt.uint32
U8 = mybir.dt.uint8
FP8X4 = mybir.dt.float8_e4m3fn_x4
RELU = mybir.ActivationFunctionType.Relu
ADD = mybir.AluOpType.add

P = 128
PACK = 4
K_PASS = P * PACK
BANK = 512

NS, ND, D0, D1 = 1024, 8192, 512, 512
PASSES = NS // K_PASS

TILES = 4
GROUP = TILES * P
GROUPS = ND // GROUP
LOAD = 4
LOADS = GROUPS // LOAD
RUN = 2
RUNS = GROUPS // RUN
FLIP_RUN = 3
AHEAD = 3
RAW_BUFS = 3
WHOLE_RUNS = 5
OUT_BUFS = 4

FLOPS = 2 * NS * D0 * D1 + 2 * ND * NS * D1


def tile_gcn_pa_t_kernel(tc, x, adj, W0, b0, out):
    nc = tc.nc
    with ExitStack() as ctx:
        ctx.enter_context(tc.manual_schedule())
        const = ctx.enter_context(tc.tile_pool(name="const", bufs=1))
        raw_pool = ctx.enter_context(tc.tile_pool(name="raw", bufs=RAW_BUFS))
        grouped_pool = ctx.enter_context(tc.tile_pool(name="grouped", bufs=FLIP_RUN + 1))
        mx_pool = ctx.enter_context(tc.tile_pool(name="mx", bufs=5))
        out_pool = ctx.enter_context(tc.tile_pool(name="outs", bufs=OUT_BUFS))
        flip_psum = ctx.enter_context(tc.psum_pool(name="flip", bufs=TILES))
        sum_psum = ctx.enter_context(tc.psum_pool(name="sums", bufs=TILES))

        ident = const.tile([P, P], F32)
        make_identity(nc, ident[:])
        bias_rows = const.tile([P, D1], BF16)
        nc.vector.memset(bias_rows[:], 0.0)
        ones = const.tile([P, P], BF16)
        nc.vector.memset(ones[:], 1.0)

        head_tile = out_pool.tile([P, RUN * TILES * D1], F32, tag="outs")
        head_raw = head_tile[:].bitcast(BF16)
        x_raw = head_raw[:, 0 : 4 * 2 * D0]
        x_view = x.rearrange("(a p e) d -> p a (e d)", a=4, p=P, e=2)
        x_halves = x_raw.rearrange("p (g a w) -> p g a w", g=PASSES, a=2)
        w_raw = head_raw[:, 4 * 2 * D0 : 4 * 2 * D0 + PACK * D1]
        nc.sync.dma_start(out=x_halves[:, 0], in_=x_view[:, 0:2, :])
        nc.sync.dma_start(out=bias_rows[0:1, :], in_=b0.rearrange("(o n) -> o n", o=1))
        nc.sync.dma_start(
            out=w_raw.rearrange("p (u w) -> p u w", u=2),
            in_=W0.rearrange("(u q e) c -> q u (e c)", u=2, q=P, e=2),
        )
        nc.sync.dma_start(out=x_halves[:, 1], in_=x_view[:, 2:4, :])

        adj_view = adj.rearrange("(c p j) k -> c p (j k)", p=P, j=LOAD * TILES)
        out_view = out.rearrange("(c p r j) n -> c r p (j n)", p=P, r=LOAD // RUN, j=RUN * TILES)
        raw, grouped, codes, scales, accs, results = {}, {}, {}, {}, {}, {}

        def load(c):
            adj_raw = raw_pool.tile([P, LOAD * TILES * NS], BF16, tag="raw")
            step = min(1 << c, LOAD) * TILES * NS
            for first in range(0, LOAD * TILES * NS, step):
                cols = slice(first, first + step)
                nc.sync.dma_start(out=adj_raw[:, cols], in_=adj_view[c][:, cols])
            raw[c] = adj_raw

        for c in range(RAW_BUFS):
            load(c)

        def flip_words(words, dest_words, engine_copy):
            bank = flip_psum.tile([P, BANK], F32, tag="flip")
            for q in range(4):
                nc.tensor.transpose(bank[:, q * P : (q + 1) * P], words[:, q * P : (q + 1) * P], ident[:])
            engine_copy(
                out=dest_words.rearrange("p (s r u) -> p s r u", s=2, u=2),
                in_=bank[:].rearrange("p (s u r) -> p s r u", s=2, u=2),
            )

        x_words = x_raw.bitcast(F32)
        x_grouped = grouped_pool.tile([P, TILES * NS], BF16, tag="grouped", align_bytes=64)
        x_grouped_words = x_grouped[:].bitcast(F32)
        x_codes = const.tile([P, NS], U32, align_bytes=64)
        x_scales = const.tile([P, NS], U8, align_bytes=64)
        w_grouped = const.tile([P, D1 * PACK], BF16, align_bytes=64)
        w_codes = const.tile([P, D1], U32, align_bytes=64)
        w_scales = const.tile([P, D1], U8, align_bytes=64)
        bias_all = const.tile([P, D1], F32)
        h_grouped = grouped_pool.tile([P, TILES * NS], BF16, tag="grouped", align_bytes=64)
        h_codes = const.tile([P, PASSES * D1], U32, align_bytes=64)
        h_scales = const.tile([P, PASSES * D1], U8, align_bytes=64)

        def flip_x(a):
            cols = slice(a * BANK, (a + 1) * BANK)
            flip_words(x_words[:, cols], x_grouped_words[:, cols], nc.scalar.copy)

        def quantise_x(g):
            nc.vector.quantize_mx(
                out=x_codes[:, g * K_PASS : (g + 1) * K_PASS].bitcast(FP8X4),
                scales=x_scales[:, g * K_PASS : (g + 1) * K_PASS],
                in_=x_grouped[:, g * PACK * K_PASS : (g + 1) * PACK * K_PASS],
            )

        def group_w(half):
            cols = slice(half * D1 // 2, (half + 1) * D1 // 2)
            nc.vector.tensor_copy(
                out=w_grouped[:].rearrange("p (c t) -> p c t", t=PACK)[:, cols, :],
                in_=w_raw.rearrange("p (t c) -> p c t", t=PACK)[:, cols, :],
            )

        def quantise_w(half):
            cols = slice(half * D1 // 2, (half + 1) * D1 // 2)
            nc.vector.quantize_mx(
                out=w_codes[:, cols].bitcast(FP8X4),
                scales=w_scales[:, cols],
                in_=w_grouped[:, half * D1 * PACK // 2 : (half + 1) * D1 * PACK // 2],
            )

        h_banks = {}

        def first_product(g, cb):
            h_bank = sum_psum.tile([P, BANK], F32, tag="sums")
            h_banks[g, cb] = h_bank
            for t in range(PACK):
                nodes = slice((PACK * g + t) * P, (PACK * g + t + 1) * P)
                nc.tensor.matmul_mx(
                    out=h_bank[:, t * P : (t + 1) * P],
                    lhsT=x_codes[:, nodes].bitcast(FP8X4),
                    lhsT_scale=x_scales[:, nodes],
                    rhs=w_codes[:, cb * P : (cb + 1) * P].bitcast(FP8X4),
                    rhs_scale=w_scales[:, cb * P : (cb + 1) * P],
                    start=True,
                    stop=True,
                )

        def add_bias(g, cb):
            first = (g * D1 + cb * P) * PACK
            nc.vector.tensor_tensor(
                out=h_grouped[:, first : first + P * PACK].rearrange("p (c t) -> p c t", t=PACK),
                in0=h_banks[g, cb][:].rearrange("p (t c) -> p c t", t=PACK),
                in1=bias_all[:, cb * P : (cb + 1) * P].unsqueeze(2).to_broadcast([P, P, PACK]),
                op=ADD,
            )

        def quantise_h(g):
            nc.vector.quantize_mx(
                out=h_codes[:, g * D1 : (g + 1) * D1].bitcast(FP8X4),
                scales=h_scales[:, g * D1 : (g + 1) * D1],
                in_=h_grouped[:, g * D1 * PACK : (g + 1) * D1 * PACK],
            )

        def flip_tile(i, j):
            if j == 0:
                adj_grouped = grouped_pool.tile([P, TILES * NS], BF16, tag="grouped", align_bytes=64)
                grouped[i] = adj_grouped
            words = raw[i // LOAD][:].bitcast(F32)
            dest = grouped[i][:].bitcast(F32)
            by_scalar = i < AHEAD or j % 2 == 1
            tile_in_load = (i % LOAD) * TILES + j
            flip_words(
                words[:, tile_in_load * BANK : (tile_in_load + 1) * BANK],
                dest[:, j * BANK : (j + 1) * BANK],
                nc.scalar.copy if by_scalar else nc.vector.tensor_copy,
            )

        def flip_group(i):
            for j in range(TILES):
                flip_tile(i, j)
            if i % LOAD == LOAD - 1 and i // LOAD + RAW_BUFS < LOADS:
                load(i // LOAD + RAW_BUFS)

        def quantise_tiles(i, first, count):
            if first == 0:
                adj_codes = mx_pool.tile([P, TILES * PASSES * P], U32, align_bytes=64)
                adj_scales = mx_pool.tile([P, TILES * PASSES * P], U8, align_bytes=64)
                codes[i], scales[i] = adj_codes, adj_scales
            cols = slice(first * PASSES * P, (first + count) * PASSES * P)
            nc.vector.quantize_mx(
                out=codes[i][:, cols].bitcast(FP8X4),
                scales=scales[i][:, cols],
                in_=grouped[i][:, first * NS : (first + count) * NS],
            )

        def multiply(i, j, g):
            if g == 0:
                acc = sum_psum.tile([P, BANK], F32, tag="sums")
                accs[i, j] = acc
            nodes = slice((j * PASSES + g) * P, (j * PASSES + g + 1) * P)
            nc.tensor.matmul_mx(
                out=accs[i, j][:],
                lhsT=codes[i][:, nodes].bitcast(FP8X4),
                lhsT_scale=scales[i][:, nodes],
                rhs=h_codes[:, g * D1 : (g + 1) * D1].bitcast(FP8X4),
                rhs_scale=h_scales[:, g * D1 : (g + 1) * D1],
                start=(g == 0),
                stop=(g == PASSES - 1),
            )

        def finish(i, j):
            tile_in_run = (i % RUN) * TILES + j
            if tile_in_run == 0:
                result = out_pool.tile([P, RUN * TILES * D1], F32, tag="outs")
                results[i // RUN] = result
            cols = slice(tile_in_run * D1, (tile_in_run + 1) * D1)
            if j == TILES - 2:
                nc.vector.tensor_relu(out=results[i // RUN][:, cols], in_=accs[i, j][:])
            else:
                nc.scalar.activation(out=results[i // RUN][:, cols], in_=accs[i, j][:], func=RELU)
            ready.append((i // RUN, tile_in_run + 1))
            if len(raw) == LOADS:
                for run, tiles in ready:
                    store(run, tiles)
                ready.clear()

        def store(run, tiles):
            if run < WHOLE_RUNS:
                piece = RUN * TILES
            elif run < RUNS - 1 or tiles <= TILES:
                piece = TILES
            else:
                piece = TILES // 2
            if tiles % piece == 0:
                cols = slice((tiles - piece) * D1, tiles * D1)
                nc.sync.dma_start(out=out_view[run * RUN // LOAD, run % (LOAD // RUN)][:, cols], in_=results[run][:, cols])

        ready = []

        def multiply_group(i):
            for j in range(TILES):
                for g in range(PASSES):
                    multiply(i, j, g)
                finish(i, j)

        flip_x(0)
        flip_x(1)
        bias_bank = sum_psum.tile([P, BANK], F32, tag="sums")
        nc.tensor.matmul(bias_bank[:], lhsT=ones[:], rhs=bias_rows[:], start=True, stop=True)
        nc.scalar.copy(out=bias_all[:], in_=bias_bank[:])
        flip_x(2)
        flip_x(3)
        group_w(0)
        quantise_w(0)
        quantise_x(0)
        first_product(0, 0)
        first_product(0, 1)
        group_w(1)
        quantise_w(1)
        first_product(0, 2)
        first_product(0, 3)
        add_bias(0, 0)
        add_bias(0, 1)
        quantise_x(1)
        flip_tile(0, 0)
        flip_tile(0, 1)
        first_product(1, 0)
        first_product(1, 1)
        add_bias(0, 2)
        add_bias(0, 3)
        flip_tile(0, 2)
        flip_tile(0, 3)
        first_product(1, 2)
        first_product(1, 3)
        add_bias(1, 0)
        quantise_h(0)
        add_bias(1, 1)
        flip_group(1)
        quantise_tiles(0, 0, 2)
        add_bias(1, 2)
        add_bias(1, 3)
        flip_group(2)
        quantise_tiles(0, 2, 2)
        quantise_h(1)
        for j in range(TILES):
            multiply(0, j, 0)
        quantise_tiles(1, 0, 2)
        quantise_tiles(1, 2, 2)
        for j in range(TILES):
            multiply(0, j, 1)
            finish(0, j)
        quantise_tiles(2, 0, TILES)
        multiply_group(1)
        done, first = AHEAD, RUN
        while first < GROUPS:
            upto = GROUPS if GROUPS - done <= FLIP_RUN + 1 else done + FLIP_RUN
            for i in range(done, upto):
                flip_group(i)
            for i in range(first, GROUPS if upto == GROUPS else upto - 1):
                if i + 1 < upto:
                    quantise_tiles(i + 1, 0, TILES)
                multiply_group(i)
            done, first = upto, GROUPS if upto == GROUPS else upto - 1
